import numpy as np
import ml_dtypes


def mxq(x, axis, fmt="e4m3"):
    dtype, down = {"e4m3": (ml_dtypes.float8_e4m3fn, 7), "e5m2": (ml_dtypes.float8_e5m2, 14)}[fmt]
    v = np.moveaxis(np.asarray(x, np.float32).astype(ml_dtypes.bfloat16).astype(np.float64), axis, -1)
    blocks = v.reshape(v.shape[:-1] + (-1, 32))
    amax = np.abs(blocks).max(-1, keepdims=True)
    byte = np.maximum(np.where(amax > 0, np.frexp(amax)[1] - 1 + 127, 0) - down, 1)
    scale = np.exp2(byte - 127.0)
    codes = (blocks / scale).astype(np.float32).astype(dtype).astype(np.float64)
    return np.moveaxis((codes * scale).reshape(v.shape), -1, axis)


WIDE = False


def mx_kscale(k):
    if not WIDE:
        return np.ones(k)
    levels = np.array([10, -10, 5, -5, 0])
    a = np.random.permutation(np.resize(levels, k // 512 * 4)).reshape(k // 512, 4)
    idx = np.arange(k)
    return np.exp2(a[idx // 512, idx % 128 // 32])


BF16 = ml_dtypes.bfloat16


def bf(x):
    return np.asarray(x, np.float32).astype(BF16)


def f64(x):
    return np.asarray(x).astype(np.float64)


E2M1 = np.array([0.0, 0.5, 1.0, 1.5, 2.0, 3.0, 4.0, 6.0, -0.0, -0.5, -1.0, -1.5, -2.0, -3.0, -4.0, -6.0])


def pack_weight(w, fmt):
    k, n = w.shape
    w = f64(bf(w)).reshape(k // 32, 32, n)
    amax = np.abs(w).max(1)
    if fmt == "e4m3":
        byte = np.frexp(amax)[1] - 1 + 127 - 7
    else:
        mant, ex = np.frexp(amax / 6.0)
        byte = np.where(mant > 0.5, ex, ex - 1) + 127
    byte = np.clip(np.where(amax > 0, byte, 1), 1, 254)
    scaled = (w * np.exp2(127.0 - byte)[:, None, :]).reshape(k, n).astype(np.float32)
    by_word = np.ascontiguousarray(scaled.reshape(k // 512, 128, 4, n).transpose(0, 1, 3, 2))
    if fmt == "e4m3":
        words = by_word.astype(ml_dtypes.float8_e4m3fn).view(np.uint8)
    else:
        c = by_word.astype(ml_dtypes.float4_e2m1fn).view(np.uint8) & 0xF
        words = c[..., 0::2] | (c[..., 1::2] << 4)
    return np.ascontiguousarray(words), np.ascontiguousarray(byte.astype(np.uint8).reshape(k // 512, 16, n))


def unpack_weight(words, scales, fmt):
    g, p, n, _ = words.shape
    if fmt == "e4m3":
        vals = np.ascontiguousarray(words).view(ml_dtypes.float8_e4m3fn).astype(np.float64)
    else:
        nib = np.empty((g, p, n, 4), np.uint8)
        nib[..., 0::2] = words & 0xF
        nib[..., 1::2] = words >> 4
        vals = E2M1[nib]
    vals = vals * np.repeat(np.exp2(scales.astype(np.float64) - 127.0), 8, axis=1)[..., None]
    return vals.transpose(0, 1, 3, 2).reshape(g * 512, n)


B, DIN, F, H, K, G = 1024, 512, 512, 512, 7, 3


def sigmoid(v):
    return 1.0 / (1.0 + np.exp(-v))


def setup_inputs():
    s = mx_kscale(DIN)
    hx = bf(np.random.standard_normal((B, DIN)) * s)
    cx2 = bf(np.random.standard_normal((B, H)))
    w1 = np.random.standard_normal((G, F, DIN)) / np.sqrt(DIN) / s
    b1 = bf(np.random.standard_normal((G, F)) * 0.5)
    w2 = np.random.standard_normal((G, H, F)) * 1.5 / np.sqrt(F)
    b2 = bf(np.random.standard_normal((G, H)) * 0.5)
    w1_words, w1_scales = pack_weight(np.swapaxes(w1, 1, 2).reshape(-1, F), "e4m3")
    w2_words, w2_scales = pack_weight(np.swapaxes(w2, 1, 2).reshape(-1, H), "e4m3")
    return {"hx": hx,
            "cx2": cx2,
            "w1_words": w1_words,
            "w1_scales": w1_scales,
            "b1": b1,
            "w2_words": w2_words,
            "w2_scales": w2_scales,
            "b2": b2}


def reference(hx, cx2, w1_words, w1_scales, b1, w2_words, w2_scales, b2):
    h1 = (mxq(f64(hx), 1, "e4m3") @ unpack_weight(w1_words, w1_scales, "e4m3").reshape(G, DIN, F)) + f64(b1)[:, None, :]
    a1 = np.tanh(h1)
    h2 = (mxq(a1, 2, "e4m3") @ unpack_weight(w2_words, w2_scales, "e4m3").reshape(G, F, H)) + f64(b2)[:, None, :]
    i2, f2, zg = sigmoid(np.tanh(h2))
    z = np.tanh(zg)
    return f2 * f64(cx2) + i2 * z

@@ -1,0 +1,199 @@
+from contextlib import ExitStack
+
+import concourse.mybir as mybir
+from concourse.masks import make_identity
+
+F32 = mybir.dt.float32
+BF16 = mybir.dt.bfloat16
+I32 = mybir.dt.int32
+U32 = mybir.dt.uint32
+U8 = mybir.dt.uint8
+FP8X4 = mybir.dt.float8_e4m3fn_x4
+FUNC = mybir.ActivationFunctionType
+ALU = mybir.AluOpType
+
+P = 128
+PACK = 4
+BATCH = 1024
+WIDTH = 512
+NETS = 3
+TILES = BATCH // P
+HALVES = 2
+HALF = BATCH // HALVES
+TILES_PER_HALF = TILES // HALVES
+SLICES = WIDTH // P
+QUADRANTS = 4
+
+FLOPS = 2 * 2 * NETS * BATCH * WIDTH * WIDTH
+
+
+def load_weight(nc, words_dram, scales_dram, words, planes):
+    for quadrant in range(QUADRANTS):
+        rows = slice(PACK * quadrant, PACK * quadrant + PACK)
+        nc.sync.dma_start(
+            out=planes[32 * quadrant : 32 * quadrant + PACK, :, :].bitcast(I32),
+            in_=scales_dram[:, rows, :].rearrange("g r n -> r g n").bitcast(I32),
+        )
+    for g in range(NETS):
+        nc.sync.dma_start(
+            out=words[:, g, :].bitcast(I32),
+            in_=words_dram[g].rearrange("p n t -> p (n t)").bitcast(I32),
+        )
+
+
+def tile_lstmcellunknowndata_pa_e_kernel(
+    tc, hx, cx2, w1_words, w1_scales, b1, w2_words, w2_scales, b2, out
+):
+    nc = tc.nc
+    with ExitStack() as stack:
+        keep = stack.enter_context(tc.tile_pool(name="keep", bufs=1))
+        stage = stack.enter_context(tc.tile_pool(name="stage", bufs=2))
+        rows_pool = stack.enter_context(tc.tile_pool(name="rows", bufs=6))
+        work = stack.enter_context(tc.tile_pool(name="work", bufs=3))
+        psum_one = stack.enter_context(tc.psum_pool(name="psum_one", bufs=4))
+        psum_two = stack.enter_context(tc.psum_pool(name="psum_two", bufs=4))
+
+        ident_f32 = keep.tile([P, P], F32)
+        make_identity(nc, ident_f32[:])
+        ident_bf16 = keep.tile([P, P], BF16)
+        make_identity(nc, ident_bf16[:])
+
+        w1_sb = keep.tile([P, NETS, WIDTH], U32, align_bytes=64)
+        w1_planes = keep.tile([P, NETS, WIDTH], U8, align_bytes=64)
+        w2_sb = keep.tile([P, NETS, WIDTH], U32, align_bytes=64)
+        w2_planes = keep.tile([P, NETS, WIDTH], U8, align_bytes=64)
+        nc.vector.memset(w1_planes[:].rearrange("p g n -> p (g n)").bitcast(I32), 0)
+        nc.vector.memset(w2_planes[:].rearrange("p g n -> p (g n)").bitcast(I32), 0)
+
+        hx_view = hx.rearrange("(p i) k -> p i k", i=TILES)
+        cx_view = cx2.rearrange("(p i) k -> p i k", i=TILES)
+        out_view = out.rearrange("(p i) k -> p i k", i=TILES)
+
+        x_sb = keep.tile([P, TILES, WIDTH], BF16)
+        for h in range(HALVES):
+            tiles = slice(h * TILES_PER_HALF, (h + 1) * TILES_PER_HALF)
+            nc.scalar.dma_start(out=x_sb[:, tiles, :], in_=hx_view[:, tiles, :])
+
+        b1_rows = keep.tile([P, P], BF16)
+        nc.vector.memset(b1_rows[:], 0.0)
+        nc.scalar.dma_start(
+            out=b1_rows[0 : NETS * SLICES, :], in_=b1.rearrange("g (j m) -> (g j) m", m=P)
+        )
+
+        load_weight(nc, w1_words, w1_scales, w1_sb, w1_planes)
+        load_weight(nc, w2_words, w2_scales, w2_sb, w2_planes)
+
+        cx_sb = keep.tile([P, TILES, WIDTH], BF16)
+        nc.gpsimd.dma_start(out=cx_sb[:], in_=cx_view)
+        b2_all = keep.tile([P, NETS, WIDTH], BF16)
+        nc.gpsimd.dma_start(
+            out=b2_all[:].rearrange("p g n -> p (g n)"),
+            in_=b2.rearrange("g n -> (g n)").partition_broadcast(P),
+        )
+
+        warm = keep.tile([P, 1], F32)
+        nc.vector.memset(warm[:], 0.0)
+        nc.scalar.activation(out=warm[:], in_=warm[:], func=FUNC.Sigmoid)
+
+        b1_ps = psum_one.tile([P, P], BF16, tag="bank")
+        nc.tensor.transpose(out=b1_ps[:], in_=b1_rows[:], identity=ident_bf16[:])
+        b1_cols = keep.tile([P, NETS * SLICES], F32)
+        nc.vector.tensor_copy(out=b1_cols[:], in_=b1_ps[:, 0 : NETS * SLICES])
+
+        hx_codes = keep.tile([P, BATCH], U32, align_bytes=64)
+        hx_scales = keep.tile([P, BATCH], U8, align_bytes=64)
+        for h in range(HALVES):
+            x_grouped = stage.tile([P, HALF, PACK], BF16, align_bytes=64)
+            grouped_words = x_grouped[:].rearrange("p c t -> p (c t)").bitcast(F32)
+            for pair in range(TILES_PER_HALF // 2):
+                xt = psum_one.tile([P, 2, 2, P], F32, tag="bank")
+                for il in range(2):
+                    i = h * TILES_PER_HALF + 2 * pair + il
+                    x_words = x_sb[:, i, :].bitcast(F32)
+                    for u in range(2):
+                        nc.tensor.transpose(
+                            out=xt[:, il, u, :],
+                            in_=x_words[:, u : WIDTH // 2 : 2],
+                            identity=ident_f32[:],
+                        )
+                nc.vector.tensor_copy(
+                    out=grouped_words[:, pair * 4 * P : (pair + 1) * 4 * P].rearrange(
+                        "p (i c u) -> p i c u", i=2, u=2
+                    ),
+                    in_=xt[:].rearrange("p i u c -> p i c u"),
+                )
+            cols = slice(h * HALF, (h + 1) * HALF)
+            nc.vector.quantize_mx(
+                out=hx_codes[:, cols].bitcast(FP8X4),
+                scales=hx_scales[:, cols],
+                in_=x_grouped[:].rearrange("p c t -> p (c t)"),
+            )
+
+        a_codes = keep.tile([P, NETS, BATCH], U32, align_bytes=64)
+        a_scales = keep.tile([P, NETS, BATCH], U8, align_bytes=64)
+        for h in range(HALVES):
+            cols = slice(h * HALF, (h + 1) * HALF)
+            for g in range(NETS):
+                a_planes = stage.tile([P, PACK, HALF], BF16)
+                for j in range(SLICES):
+                    units = slice(j * P, (j + 1) * P)
+                    h1 = psum_one.tile([P, HALF], F32, tag="bank")
+                    nc.tensor.matmul_mx(
+                        out=h1[:],
+                        lhsT=w1_sb[:, g, units].bitcast(FP8X4),
+                        lhsT_scale=w1_planes[:, g, units],
+                        rhs=hx_codes[:, cols].bitcast(FP8X4),
+                        rhs_scale=hx_scales[:, cols],
+                        start=True,
+                        stop=True,
+                    )
+                    a_rows = rows_pool.tile([P, HALF], BF16)
+                    column = g * SLICES + j
+                    nc.scalar.activation(
+                        out=a_rows[:],
+                        in_=h1[:],
+                        func=FUNC.Tanh,
+                        bias=b1_cols[:, column : column + 1],
+                    )
+                    nc.sync.dma_start(out=a_planes[32 * j : 32 * j + 32, :, :], in_=a_rows[:])
+                a_grouped = stage.tile([P, HALF, PACK], BF16, align_bytes=64)
+                nc.vector.tensor_copy(
+                    out=a_grouped[:], in_=a_planes[:].rearrange("p t c -> p c t")
+                )
+                nc.vector.quantize_mx(
+                    out=a_codes[:, g, cols].bitcast(FP8X4),
+                    scales=a_scales[:, g, cols],
+                    in_=a_grouped[:].rearrange("p c t -> p (c t)"),
+                )
+
+        for i in range(TILES):
+            rows = slice(i * P, (i + 1) * P)
+            gates = work.tile([P, NETS, WIDTH], F32)
+            for g in range(NETS):
+                h2 = psum_two.tile([P, WIDTH], F32)
+                nc.tensor.matmul_mx(
+                    out=h2[:],
+                    lhsT=a_codes[:, g, rows].bitcast(FP8X4),
+                    lhsT_scale=a_scales[:, g, rows],
+                    rhs=w2_sb[:, g, :].bitcast(FP8X4),
+                    rhs_scale=w2_planes[:, g, :],
+                    start=True,
+                    stop=True,
+                )
+                nc.vector.tensor_tensor(
+                    out=gates[:, g, :], in0=h2[:], in1=b2_all[:, g, :], op=ALU.add
+                )
+            flat = gates[:].rearrange("p g n -> p (g n)")
+            nc.scalar.activation(out=flat, in_=flat, func=FUNC.Tanh)
+            nc.scalar.activation(out=flat, in_=flat, func=FUNC.Sigmoid)
+            candidate = work.tile([P, WIDTH], F32)
+            nc.scalar.activation(out=candidate[:], in_=gates[:, 2, :], func=FUNC.Tanh)
+            cell = work.tile([P, WIDTH], F32)
+            nc.vector.tensor_tensor(
+                out=cell[:], in0=gates[:, 1, :], in1=cx_sb[:, i, :], op=ALU.mult
+            )
+            nc.vector.tensor_tensor(
+                out=candidate[:], in0=gates[:, 0, :], in1=candidate[:], op=ALU.mult
+            )
+            nc.vector.tensor_tensor(out=cell[:], in0=cell[:], in1=candidate[:], op=ALU.add)
+            nc.sync.dma_start(out=out_view[:, i, :], in_=cell[:])

@@ -23,6 +23,7 @@ HALF = BATCH // HALVES
 TILES_PER_HALF = TILES // HALVES
 SLICES = WIDTH // P
 QUADRANTS = 4
+CHUNKS = HALVES * SLICES
 
 FLOPS = 2 * 2 * NETS * BATCH * WIDTH * WIDTH
 
@@ -48,21 +49,19 @@ def tile_lstmcellunknowndata_pa_e_kernel(
     with ExitStack() as stack:
         keep = stack.enter_context(tc.tile_pool(name="keep", bufs=1))
         stage = stack.enter_context(tc.tile_pool(name="stage", bufs=2))
-        rows_pool = stack.enter_context(tc.tile_pool(name="rows", bufs=6))
-        work = stack.enter_context(tc.tile_pool(name="work", bufs=3))
-        psum_one = stack.enter_context(tc.psum_pool(name="psum_one", bufs=4))
-        psum_two = stack.enter_context(tc.psum_pool(name="psum_two", bufs=4))
-
-        ident_f32 = keep.tile([P, P], F32)
-        make_identity(nc, ident_f32[:])
-        ident_bf16 = keep.tile([P, P], BF16)
-        make_identity(nc, ident_bf16[:])
+        rows_pool = stack.enter_context(tc.tile_pool(name="rows", bufs=12))
+        planes_pool = stack.enter_context(tc.tile_pool(name="planes", bufs=4))
+        work = stack.enter_context(tc.tile_pool(name="work", bufs=4))
+        psum_sums = stack.enter_context(tc.psum_pool(name="psum_sums", bufs=4))
+        psum_turn = stack.enter_context(tc.psum_pool(name="psum_turn", bufs=4))
 
         w1_sb = keep.tile([P, NETS, WIDTH], U32, align_bytes=64)
         w1_planes = keep.tile([P, NETS, WIDTH], U8, align_bytes=64)
         w2_sb = keep.tile([P, NETS, WIDTH], U32, align_bytes=64)
         w2_planes = keep.tile([P, NETS, WIDTH], U8, align_bytes=64)
         nc.vector.memset(w1_planes[:].rearrange("p g n -> p (g n)").bitcast(I32), 0)
+        bias_rows = keep.tile([P, P], BF16)
+        nc.vector.memset(bias_rows[:], 0.0)
         nc.vector.memset(w2_planes[:].rearrange("p g n -> p (g n)").bitcast(I32), 0)
 
         hx_view = hx.rearrange("(p i) k -> p i k", i=TILES)
@@ -70,74 +69,78 @@ def tile_lstmcellunknowndata_pa_e_kernel(
         out_view = out.rearrange("(p i) k -> p i k", i=TILES)
 
         x_sb = keep.tile([P, TILES, WIDTH], BF16)
-        for h in range(HALVES):
-            tiles = slice(h * TILES_PER_HALF, (h + 1) * TILES_PER_HALF)
+        for pair in range(TILES // 2):
+            tiles = slice(2 * pair, 2 * pair + 2)
             nc.scalar.dma_start(out=x_sb[:, tiles, :], in_=hx_view[:, tiles, :])
-
-        b1_rows = keep.tile([P, P], BF16)
-        nc.vector.memset(b1_rows[:], 0.0)
-        nc.scalar.dma_start(
-            out=b1_rows[0 : NETS * SLICES, :], in_=b1.rearrange("g (j m) -> (g j) m", m=P)
-        )
 
         load_weight(nc, w1_words, w1_scales, w1_sb, w1_planes)
         load_weight(nc, w2_words, w2_scales, w2_sb, w2_planes)
 
+        ident_f32 = keep.tile([P, P], F32)
+        make_identity(nc, ident_f32[:])
+        rows_of_a_bias = NETS * SLICES
+        nc.gpsimd.dma_start(
+            out=bias_rows[0:rows_of_a_bias, :], in_=b1.rearrange("g (j m) -> (g j) m", m=P)
+        )
+        nc.gpsimd.dma_start(
+            out=bias_rows[rows_of_a_bias : 2 * rows_of_a_bias, :],
+            in_=b2.rearrange("g (j m) -> (g j) m", m=P),
+        )
+        ident_bf16 = keep.tile([P, P], BF16)
+        make_identity(nc, ident_bf16[:])
         cx_sb = keep.tile([P, TILES, WIDTH], BF16)
         nc.gpsimd.dma_start(out=cx_sb[:], in_=cx_view)
-        b2_all = keep.tile([P, NETS, WIDTH], BF16)
-        nc.gpsimd.dma_start(
-            out=b2_all[:].rearrange("p g n -> p (g n)"),
-            in_=b2.rearrange("g n -> (g n)").partition_broadcast(P),
-        )
 
         warm = keep.tile([P, 1], F32)
         nc.vector.memset(warm[:], 0.0)
         nc.scalar.activation(out=warm[:], in_=warm[:], func=FUNC.Sigmoid)
 
-        b1_ps = psum_one.tile([P, P], BF16, tag="bank")
-        nc.tensor.transpose(out=b1_ps[:], in_=b1_rows[:], identity=ident_bf16[:])
-        b1_cols = keep.tile([P, NETS * SLICES], F32)
-        nc.vector.tensor_copy(out=b1_cols[:], in_=b1_ps[:, 0 : NETS * SLICES])
-
         hx_codes = keep.tile([P, BATCH], U32, align_bytes=64)
         hx_scales = keep.tile([P, BATCH], U8, align_bytes=64)
-        for h in range(HALVES):
-            x_grouped = stage.tile([P, HALF, PACK], BF16, align_bytes=64)
-            grouped_words = x_grouped[:].rearrange("p c t -> p (c t)").bitcast(F32)
-            for pair in range(TILES_PER_HALF // 2):
-                xt = psum_one.tile([P, 2, 2, P], F32, tag="bank")
-                for il in range(2):
-                    i = h * TILES_PER_HALF + 2 * pair + il
-                    x_words = x_sb[:, i, :].bitcast(F32)
-                    for u in range(2):
-                        nc.tensor.transpose(
-                            out=xt[:, il, u, :],
-                            in_=x_words[:, u : WIDTH // 2 : 2],
-                            identity=ident_f32[:],
-                        )
-                nc.vector.tensor_copy(
-                    out=grouped_words[:, pair * 4 * P : (pair + 1) * 4 * P].rearrange(
-                        "p (i c u) -> p i c u", i=2, u=2
-                    ),
-                    in_=xt[:].rearrange("p i u c -> p i c u"),
-                )
-            cols = slice(h * HALF, (h + 1) * HALF)
+
+        def quantise_hx(pair):
+            xt = psum_turn.tile([P, 2, 2, P], F32, tag="turn")
+            for il in range(2):
+                x_words = x_sb[:, 2 * pair + il, :].bitcast(F32)
+                for u in range(2):
+                    nc.tensor.transpose(
+                        out=xt[:, il, u, :],
+                        in_=x_words[:, u : WIDTH // 2 : 2],
+                        identity=ident_f32[:],
+                    )
+            x_grouped = stage.tile([P, 2 * P, PACK], BF16, align_bytes=64)
+            nc.vector.tensor_copy(
+                out=x_grouped[:]
+                .rearrange("p c t -> p (c t)")
+                .bitcast(F32)
+                .rearrange("p (i c u) -> p i c u", i=2, u=2),
+                in_=xt[:].rearrange("p i u c -> p i c u"),
+            )
+            cols = slice(pair * 2 * P, (pair + 1) * 2 * P)
             nc.vector.quantize_mx(
                 out=hx_codes[:, cols].bitcast(FP8X4),
                 scales=hx_scales[:, cols],
                 in_=x_grouped[:].rearrange("p c t -> p (c t)"),
             )
 
+        quantise_hx(0)
+        quantise_hx(1)
+
+        bias_ps = psum_turn.tile([P, P], BF16, tag="turn")
+        nc.tensor.transpose(out=bias_ps[:], in_=bias_rows[:], identity=ident_bf16[:])
+        bias_cols = keep.tile([P, 2 * rows_of_a_bias], F32)
+        nc.vector.tensor_copy(out=bias_cols[:], in_=bias_ps[:, 0 : 2 * rows_of_a_bias])
+
         a_codes = keep.tile([P, NETS, BATCH], U32, align_bytes=64)
         a_scales = keep.tile([P, NETS, BATCH], U8, align_bytes=64)
-        for h in range(HALVES):
+
+        def layer_one(h):
             cols = slice(h * HALF, (h + 1) * HALF)
             for g in range(NETS):
-                a_planes = stage.tile([P, PACK, HALF], BF16)
+                a_planes = planes_pool.tile([P, PACK, HALF], BF16)
                 for j in range(SLICES):
                     units = slice(j * P, (j + 1) * P)
-                    h1 = psum_one.tile([P, HALF], F32, tag="bank")
+                    h1 = psum_sums.tile([P, HALF], F32, tag="sums")
                     nc.tensor.matmul_mx(
                         out=h1[:],
                         lhsT=w1_sb[:, g, units].bitcast(FP8X4),
@@ -153,12 +156,13 @@ def tile_lstmcellunknowndata_pa_e_kernel(
                         out=a_rows[:],
                         in_=h1[:],
                         func=FUNC.Tanh,
-                        bias=b1_cols[:, column : column + 1],
+                        bias=bias_cols[:, column : column + 1],
                     )
                     nc.sync.dma_start(out=a_planes[32 * j : 32 * j + 32, :, :], in_=a_rows[:])
                 a_grouped = stage.tile([P, HALF, PACK], BF16, align_bytes=64)
                 nc.vector.tensor_copy(
-                    out=a_grouped[:], in_=a_planes[:].rearrange("p t c -> p c t")
+                    out=a_grouped[:].rearrange("p (c i) t -> p c t i", i=4),
+                    in_=a_planes[:].rearrange("p t (c i) -> p c t i", i=4),
                 )
                 nc.vector.quantize_mx(
                     out=a_codes[:, g, cols].bitcast(FP8X4),
@@ -166,34 +170,81 @@ def tile_lstmcellunknowndata_pa_e_kernel(
                     in_=a_grouped[:].rearrange("p c t -> p (c t)"),
                 )
 
-        for i in range(TILES):
-            rows = slice(i * P, (i + 1) * P)
-            gates = work.tile([P, NETS, WIDTH], F32)
+        layer_one(0)
+        quantise_hx(2)
+        quantise_hx(3)
+        layer_one(1)
+
+        turned_tanh_of = {}
+        gates_of = {}
+        cell_of = {}
+
+        def second_layer_tanh(chunk):
+            h, j = divmod(chunk, SLICES)
+            cols = slice(h * HALF, (h + 1) * HALF)
+            units = slice(j * P, (j + 1) * P)
+            turned_tanh = work.tile([P, NETS, HALF], F32, name="turned_tanh")
+            turned_tanh_of[chunk] = turned_tanh
             for g in range(NETS):
-                h2 = psum_two.tile([P, WIDTH], F32)
+                h2 = psum_sums.tile([P, HALF], F32, tag="sums")
                 nc.tensor.matmul_mx(
                     out=h2[:],
-                    lhsT=a_codes[:, g, rows].bitcast(FP8X4),
-                    lhsT_scale=a_scales[:, g, rows],
-                    rhs=w2_sb[:, g, :].bitcast(FP8X4),
-                    rhs_scale=w2_planes[:, g, :],
+                    lhsT=w2_sb[:, g, units].bitcast(FP8X4),
+                    lhsT_scale=w2_planes[:, g, units],
+                    rhs=a_codes[:, g, cols].bitcast(FP8X4),
+                    rhs_scale=a_scales[:, g, cols],
                     start=True,
                     stop=True,
                 )
-                nc.vector.tensor_tensor(
-                    out=gates[:, g, :], in0=h2[:], in1=b2_all[:, g, :], op=ALU.add
+                column = rows_of_a_bias + g * SLICES + j
+                nc.scalar.activation(
+                    out=turned_tanh[:, g, :],
+                    in_=h2[:],
+                    func=FUNC.Tanh,
+                    bias=bias_cols[:, column : column + 1],
                 )
-            flat = gates[:].rearrange("p g n -> p (g n)")
-            nc.scalar.activation(out=flat, in_=flat, func=FUNC.Tanh)
-            nc.scalar.activation(out=flat, in_=flat, func=FUNC.Sigmoid)
-            candidate = work.tile([P, WIDTH], F32)
-            nc.scalar.activation(out=candidate[:], in_=gates[:, 2, :], func=FUNC.Tanh)
-            cell = work.tile([P, WIDTH], F32)
+
+        def turn_back_and_sigmoid(chunk):
+            h, j = divmod(chunk, SLICES)
+            turned_tanh = turned_tanh_of[chunk]
+            gates = work.tile([P, NETS, TILES_PER_HALF, P], F32, name="gates")
+            gates_of[chunk] = gates
+            for g in range(NETS):
+                back = psum_turn.tile([P, TILES_PER_HALF, P], F32, tag="turn")
+                for il in range(TILES_PER_HALF):
+                    nc.tensor.transpose(
+                        out=back[:, il, :],
+                        in_=turned_tanh[:, g, il * P : (il + 1) * P],
+                        identity=ident_f32[:],
+                    )
+                nc.scalar.activation(out=gates[:, g, :, :], in_=back[:], func=FUNC.Sigmoid)
+            cell = work.tile([P, TILES_PER_HALF, P], F32, name="cell")
+            cell_of[chunk] = cell
+            tiles = slice(h * TILES_PER_HALF, (h + 1) * TILES_PER_HALF)
             nc.vector.tensor_tensor(
-                out=cell[:], in0=gates[:, 1, :], in1=cx_sb[:, i, :], op=ALU.mult
+                out=cell[:],
+                in0=gates[:, 1, :, :],
+                in1=cx_sb[:, tiles, j * P : (j + 1) * P],
+                op=ALU.mult,
             )
+
+        def finish(chunk):
+            h, j = divmod(chunk, SLICES)
+            gates = gates_of[chunk]
+            cell = cell_of[chunk]
+            candidate = work.tile([P, TILES_PER_HALF, P], F32)
+            nc.scalar.activation(out=candidate[:], in_=gates[:, 2, :, :], func=FUNC.Tanh)
             nc.vector.tensor_tensor(
-                out=candidate[:], in0=gates[:, 0, :], in1=candidate[:], op=ALU.mult
+                out=candidate[:], in0=gates[:, 0, :, :], in1=candidate[:], op=ALU.mult
             )
             nc.vector.tensor_tensor(out=cell[:], in0=cell[:], in1=candidate[:], op=ALU.add)
-            nc.sync.dma_start(out=out_view[:, i, :], in_=cell[:])
+            tiles = slice(h * TILES_PER_HALF, (h + 1) * TILES_PER_HALF)
+            nc.sync.dma_start(out=out_view[:, tiles, j * P : (j + 1) * P], in_=cell[:])
+
+        for step in range(CHUNKS + 2):
+            if step < CHUNKS:
+                second_layer_tanh(step)
+            if 1 <= step <= CHUNKS:
+                turn_back_and_sigmoid(step - 1)
+            if step >= 2:
+                finish(step - 2)

@@ -54,6 +54,7 @@ def tile_lstmcellunknowndata_pa_e_kernel(
         work = stack.enter_context(tc.tile_pool(name="work", bufs=4))
         psum_sums = stack.enter_context(tc.psum_pool(name="psum_sums", bufs=4))
         psum_turn = stack.enter_context(tc.psum_pool(name="psum_turn", bufs=4))
+        stack.enter_context(tc.manual_schedule())
 
         w1_sb = keep.tile([P, NETS, WIDTH], U32, align_bytes=64)
         w1_planes = keep.tile([P, NETS, WIDTH], U8, align_bytes=64)
@@ -134,46 +135,55 @@ def tile_lstmcellunknowndata_pa_e_kernel(
         a_codes = keep.tile([P, NETS, BATCH], U32, align_bytes=64)
         a_scales = keep.tile([P, NETS, BATCH], U8, align_bytes=64)
 
-        def layer_one(h):
-            cols = slice(h * HALF, (h + 1) * HALF)
-            for g in range(NETS):
-                a_planes = planes_pool.tile([P, PACK, HALF], BF16)
-                for j in range(SLICES):
-                    units = slice(j * P, (j + 1) * P)
-                    h1 = psum_sums.tile([P, HALF], F32, tag="sums")
-                    nc.tensor.matmul_mx(
-                        out=h1[:],
-                        lhsT=w1_sb[:, g, units].bitcast(FP8X4),
-                        lhsT_scale=w1_planes[:, g, units],
-                        rhs=hx_codes[:, cols].bitcast(FP8X4),
-                        rhs_scale=hx_scales[:, cols],
-                        start=True,
-                        stop=True,
-                    )
-                    a_rows = rows_pool.tile([P, HALF], BF16)
-                    column = g * SLICES + j
-                    nc.scalar.activation(
-                        out=a_rows[:],
-                        in_=h1[:],
-                        func=FUNC.Tanh,
-                        bias=bias_cols[:, column : column + 1],
-                    )
-                    nc.sync.dma_start(out=a_planes[32 * j : 32 * j + 32, :, :], in_=a_rows[:])
-                a_grouped = stage.tile([P, HALF, PACK], BF16, align_bytes=64)
-                nc.vector.tensor_copy(
-                    out=a_grouped[:].rearrange("p (c i) t -> p c t i", i=4),
-                    in_=a_planes[:].rearrange("p t (c i) -> p c t i", i=4),
-                )
-                nc.vector.quantize_mx(
-                    out=a_codes[:, g, cols].bitcast(FP8X4),
-                    scales=a_scales[:, g, cols],
-                    in_=a_grouped[:].rearrange("p c t -> p (c t)"),
-                )
+        a_planes_of = {}
 
-        layer_one(0)
+        def first_layer_tanh(h, g):
+            cols = slice(h * HALF, (h + 1) * HALF)
+            a_planes = planes_pool.tile([P, PACK, HALF], BF16, name="a_planes")
+            a_planes_of[(h, g)] = a_planes
+            for j in range(SLICES):
+                units = slice(j * P, (j + 1) * P)
+                h1 = psum_sums.tile([P, HALF], F32, tag="sums")
+                nc.tensor.matmul_mx(
+                    out=h1[:],
+                    lhsT=w1_sb[:, g, units].bitcast(FP8X4),
+                    lhsT_scale=w1_planes[:, g, units],
+                    rhs=hx_codes[:, cols].bitcast(FP8X4),
+                    rhs_scale=hx_scales[:, cols],
+                    start=True,
+                    stop=True,
+                )
+                a_rows = rows_pool.tile([P, HALF], BF16)
+                column = g * SLICES + j
+                nc.scalar.activation(
+                    out=a_rows[:],
+                    in_=h1[:],
+                    func=FUNC.Tanh,
+                    bias=bias_cols[:, column : column + 1],
+                )
+                nc.sync.dma_start(out=a_planes[32 * j : 32 * j + 32, :, :], in_=a_rows[:])
+
+        def quantise_a(h, g):
+            cols = slice(h * HALF, (h + 1) * HALF)
+            a_planes = a_planes_of[(h, g)]
+            a_grouped = stage.tile([P, HALF, PACK], BF16, align_bytes=64)
+            nc.vector.tensor_copy(
+                out=a_grouped[:].rearrange("p (c i) t -> p c t i", i=4),
+                in_=a_planes[:].rearrange("p t (c i) -> p c t i", i=4),
+            )
+            nc.vector.quantize_mx(
+                out=a_codes[:, g, cols].bitcast(FP8X4),
+                scales=a_scales[:, g, cols],
+                in_=a_grouped[:].rearrange("p c t -> p (c t)"),
+            )
+
+        first_layer_tanh(0, 0)
         quantise_hx(2)
         quantise_hx(3)
-        layer_one(1)
+        quantise_a(0, 0)
+        for h, g in ((0, 1), (0, 2), (1, 0), (1, 1), (1, 2)):
+            first_layer_tanh(h, g)
+            quantise_a(h, g)
 
         turned_tanh_of = {}
         gates_of = {}

@@ -21,6 +21,7 @@ TILES = BATCH // P
 HALVES = 2
 HALF = BATCH // HALVES
 TILES_PER_HALF = TILES // HALVES
+PAIR = 2 * P
 SLICES = WIDTH // P
 QUADRANTS = 4
 CHUNKS = HALVES * SLICES
@@ -28,18 +29,20 @@ CHUNKS = HALVES * SLICES
 FLOPS = 2 * 2 * NETS * BATCH * WIDTH * WIDTH
 
 
-def load_weight(nc, words_dram, scales_dram, words, planes):
+def load_scales(nc, scales_dram, planes):
     for quadrant in range(QUADRANTS):
         rows = slice(PACK * quadrant, PACK * quadrant + PACK)
         nc.sync.dma_start(
             out=planes[32 * quadrant : 32 * quadrant + PACK, :, :].bitcast(I32),
             in_=scales_dram[:, rows, :].rearrange("g r n -> r g n").bitcast(I32),
         )
-    for g in range(NETS):
-        nc.sync.dma_start(
-            out=words[:, g, :].bitcast(I32),
-            in_=words_dram[g].rearrange("p n t -> p (n t)").bitcast(I32),
-        )
+
+
+def load_words(nc, words_dram, words, nets):
+    nc.sync.dma_start(
+        out=words[:, nets, :].bitcast(I32),
+        in_=words_dram[nets].rearrange("g p n t -> p g (n t)").bitcast(I32),
+    )
 
 
 def tile_lstmcellunknowndata_pa_e_kernel(
@@ -60,40 +63,39 @@ def tile_lstmcellunknowndata_pa_e_kernel(
         w1_planes = keep.tile([P, NETS, WIDTH], U8, align_bytes=64)
         w2_sb = keep.tile([P, NETS, WIDTH], U32, align_bytes=64)
         w2_planes = keep.tile([P, NETS, WIDTH], U8, align_bytes=64)
+        b1_rows = keep.tile([P, P], BF16)
+        b2_rows = keep.tile([P, P], BF16)
+        warm = keep.tile([P, 1], F32)
         nc.vector.memset(w1_planes[:].rearrange("p g n -> p (g n)").bitcast(I32), 0)
-        bias_rows = keep.tile([P, P], BF16)
-        nc.vector.memset(bias_rows[:], 0.0)
+        nc.vector.memset(b1_rows[:], 0.0)
+        nc.vector.memset(warm[:], 0.0)
+        nc.vector.memset(b2_rows[:], 0.0)
         nc.vector.memset(w2_planes[:].rearrange("p g n -> p (g n)").bitcast(I32), 0)
+
+        ident_f32 = keep.tile([P, P], F32)
+        make_identity(nc, ident_f32[:])
+        ident_bf16 = keep.tile([P, P], BF16)
+        make_identity(nc, ident_bf16[:])
 
         hx_view = hx.rearrange("(p i) k -> p i k", i=TILES)
         cx_view = cx2.rearrange("(p i) k -> p i k", i=TILES)
         out_view = out.rearrange("(p i) k -> p i k", i=TILES)
-
         x_sb = keep.tile([P, TILES, WIDTH], BF16)
-        for pair in range(TILES // 2):
-            tiles = slice(2 * pair, 2 * pair + 2)
-            nc.scalar.dma_start(out=x_sb[:, tiles, :], in_=hx_view[:, tiles, :])
-
-        load_weight(nc, w1_words, w1_scales, w1_sb, w1_planes)
-        load_weight(nc, w2_words, w2_scales, w2_sb, w2_planes)
-
-        ident_f32 = keep.tile([P, P], F32)
-        make_identity(nc, ident_f32[:])
-        rows_of_a_bias = NETS * SLICES
-        nc.gpsimd.dma_start(
-            out=bias_rows[0:rows_of_a_bias, :], in_=b1.rearrange("g (j m) -> (g j) m", m=P)
-        )
-        nc.gpsimd.dma_start(
-            out=bias_rows[rows_of_a_bias : 2 * rows_of_a_bias, :],
-            in_=b2.rearrange("g (j m) -> (g j) m", m=P),
-        )
-        ident_bf16 = keep.tile([P, P], BF16)
-        make_identity(nc, ident_bf16[:])
         cx_sb = keep.tile([P, TILES, WIDTH], BF16)
+        bias_rows = NETS * SLICES
+
+        nc.scalar.dma_start(out=x_sb[:, 0:2, :], in_=hx_view[:, 0:2, :])
+        nc.scalar.dma_start(out=x_sb[:, 2:4, :], in_=hx_view[:, 2:4, :])
+        load_scales(nc, w1_scales, w1_planes)
+        load_words(nc, w1_words, w1_sb, slice(0, 1))
+        nc.scalar.dma_start(out=b1_rows[0:bias_rows, :], in_=b1.rearrange("g (j m) -> (g j) m", m=P))
+        load_words(nc, w1_words, w1_sb, slice(1, NETS))
+        nc.sync.dma_start(out=x_sb[:, 4:8, :], in_=hx_view[:, 4:8, :])
+        nc.sync.dma_start(out=b2_rows[0:bias_rows, :], in_=b2.rearrange("g (j m) -> (g j) m", m=P))
+        load_scales(nc, w2_scales, w2_planes)
+        load_words(nc, w2_words, w2_sb, slice(0, NETS))
         nc.gpsimd.dma_start(out=cx_sb[:], in_=cx_view)
 
-        warm = keep.tile([P, 1], F32)
-        nc.vector.memset(warm[:], 0.0)
         nc.scalar.activation(out=warm[:], in_=warm[:], func=FUNC.Sigmoid)
 
         hx_codes = keep.tile([P, BATCH], U32, align_bytes=64)
@@ -109,7 +111,7 @@ def tile_lstmcellunknowndata_pa_e_kernel(
                         in_=x_words[:, u : WIDTH // 2 : 2],
                         identity=ident_f32[:],
                     )
-            x_grouped = stage.tile([P, 2 * P, PACK], BF16, align_bytes=64)
+            x_grouped = stage.tile([P, PAIR, PACK], BF16, align_bytes=64)
             nc.vector.tensor_copy(
                 out=x_grouped[:]
                 .rearrange("p c t -> p (c t)")
@@ -117,33 +119,34 @@ def tile_lstmcellunknowndata_pa_e_kernel(
                 .rearrange("p (i c u) -> p i c u", i=2, u=2),
                 in_=xt[:].rearrange("p i u c -> p i c u"),
             )
-            cols = slice(pair * 2 * P, (pair + 1) * 2 * P)
+            cols = slice(pair * PAIR, (pair + 1) * PAIR)
             nc.vector.quantize_mx(
                 out=hx_codes[:, cols].bitcast(FP8X4),
                 scales=hx_scales[:, cols],
                 in_=x_grouped[:].rearrange("p c t -> p (c t)"),
             )
 
-        quantise_hx(0)
-        quantise_hx(1)
-
-        bias_ps = psum_turn.tile([P, P], BF16, tag="turn")
-        nc.tensor.transpose(out=bias_ps[:], in_=bias_rows[:], identity=ident_bf16[:])
-        bias_cols = keep.tile([P, 2 * rows_of_a_bias], F32)
-        nc.vector.tensor_copy(out=bias_cols[:], in_=bias_ps[:, 0 : 2 * rows_of_a_bias])
+        def bias_columns(rows, name):
+            turned = psum_turn.tile([P, P], BF16, tag="turn")
+            nc.tensor.transpose(out=turned[:], in_=rows[:], identity=ident_bf16[:])
+            columns = keep.tile([P, bias_rows], F32, name=name)
+            nc.vector.tensor_copy(out=columns[:], in_=turned[:, 0:bias_rows])
+            return columns
 
         a_codes = keep.tile([P, NETS, BATCH], U32, align_bytes=64)
         a_scales = keep.tile([P, NETS, BATCH], U8, align_bytes=64)
-
         a_planes_of = {}
 
-        def first_layer_tanh(h, g):
-            cols = slice(h * HALF, (h + 1) * HALF)
-            a_planes = planes_pool.tile([P, PACK, HALF], BF16, name="a_planes")
-            a_planes_of[(h, g)] = a_planes
+        def first_layer_tanh(g, first_col, n_cols):
+            h = first_col // HALF
+            if (h, g) not in a_planes_of:
+                a_planes_of[(h, g)] = planes_pool.tile([P, PACK, HALF], BF16, name="a_planes")
+            a_planes = a_planes_of[(h, g)]
+            cols = slice(first_col, first_col + n_cols)
+            cols_in_half = slice(first_col - h * HALF, first_col - h * HALF + n_cols)
             for j in range(SLICES):
                 units = slice(j * P, (j + 1) * P)
-                h1 = psum_sums.tile([P, HALF], F32, tag="sums")
+                h1 = psum_sums.tile([P, n_cols], F32, tag="sums")
                 nc.tensor.matmul_mx(
                     out=h1[:],
                     lhsT=w1_sb[:, g, units].bitcast(FP8X4),
@@ -153,23 +156,21 @@ def tile_lstmcellunknowndata_pa_e_kernel(
                     start=True,
                     stop=True,
                 )
-                a_rows = rows_pool.tile([P, HALF], BF16)
+                a_rows = rows_pool.tile([P, n_cols], BF16, tag="a_rows")
                 column = g * SLICES + j
                 nc.scalar.activation(
-                    out=a_rows[:],
-                    in_=h1[:],
-                    func=FUNC.Tanh,
-                    bias=bias_cols[:, column : column + 1],
+                    out=a_rows[:], in_=h1[:], func=FUNC.Tanh, bias=b1_cols[:, column : column + 1]
                 )
-                nc.sync.dma_start(out=a_planes[32 * j : 32 * j + 32, :, :], in_=a_rows[:])
+                nc.sync.dma_start(
+                    out=a_planes[32 * j : 32 * j + 32, :, cols_in_half], in_=a_rows[:]
+                )
 
         def quantise_a(h, g):
             cols = slice(h * HALF, (h + 1) * HALF)
-            a_planes = a_planes_of[(h, g)]
             a_grouped = stage.tile([P, HALF, PACK], BF16, align_bytes=64)
             nc.vector.tensor_copy(
                 out=a_grouped[:].rearrange("p (c i) t -> p c t i", i=4),
-                in_=a_planes[:].rearrange("p t (c i) -> p c t i", i=4),
+                in_=a_planes_of[(h, g)][:].rearrange("p t (c i) -> p c t i", i=4),
             )
             nc.vector.quantize_mx(
                 out=a_codes[:, g, cols].bitcast(FP8X4),
@@ -177,12 +178,17 @@ def tile_lstmcellunknowndata_pa_e_kernel(
                 in_=a_grouped[:].rearrange("p c t -> p (c t)"),
             )
 
-        first_layer_tanh(0, 0)
+        quantise_hx(0)
+        b1_cols = bias_columns(b1_rows, "b1_cols")
+        quantise_hx(1)
+        first_layer_tanh(0, 0, PAIR)
+        first_layer_tanh(0, PAIR, PAIR)
         quantise_hx(2)
         quantise_hx(3)
+        b2_cols = bias_columns(b2_rows, "b2_cols")
         quantise_a(0, 0)
         for h, g in ((0, 1), (0, 2), (1, 0), (1, 1), (1, 2)):
-            first_layer_tanh(h, g)
+            first_layer_tanh(g, h * HALF, HALF)
             quantise_a(h, g)
 
         turned_tanh_of = {}
@@ -206,12 +212,12 @@ def tile_lstmcellunknowndata_pa_e_kernel(
                     start=True,
                     stop=True,
                 )
-                column = rows_of_a_bias + g * SLICES + j
+                column = g * SLICES + j
                 nc.scalar.activation(
                     out=turned_tanh[:, g, :],
                     in_=h2[:],
                     func=FUNC.Tanh,
-                    bias=bias_cols[:, column : column + 1],
+                    bias=b2_cols[:, column : column + 1],
                 )
 
         def turn_back_and_sigmoid(chunk):
@@ -219,7 +225,7 @@ def tile_lstmcellunknowndata_pa_e_kernel(
             turned_tanh = turned_tanh_of[chunk]
             gates = work.tile([P, NETS, TILES_PER_HALF, P], F32, name="gates")
             gates_of[chunk] = gates
-            for g in range(NETS):
+            for g in reversed(range(NETS)):
                 back = psum_turn.tile([P, TILES_PER_HALF, P], F32, tag="turn")
                 for il in range(TILES_PER_HALF):
                     nc.tensor.transpose(
@@ -252,9 +258,9 @@ def tile_lstmcellunknowndata_pa_e_kernel(
             nc.sync.dma_start(out=out_view[:, tiles, j * P : (j + 1) * P], in_=cell[:])
 
         for step in range(CHUNKS + 2):
+            if step >= 2:
+                finish(step - 2)
             if step < CHUNKS:
                 second_layer_tanh(step)
             if 1 <= step <= CHUNKS:
                 turn_back_and_sigmoid(step - 1)
-            if step >= 2:
-                finish(step - 2)

@@ -89,8 +89,9 @@ def tile_lstmcellunknowndata_pa_e_kernel(
         load_scales(nc, w1_scales, w1_planes)
         load_words(nc, w1_words, w1_sb, slice(0, 1))
         nc.scalar.dma_start(out=b1_rows[0:bias_rows, :], in_=b1.rearrange("g (j m) -> (g j) m", m=P))
-        load_words(nc, w1_words, w1_sb, slice(1, NETS))
+        load_words(nc, w1_words, w1_sb, slice(1, 2))
         nc.sync.dma_start(out=x_sb[:, 4:8, :], in_=hx_view[:, 4:8, :])
+        load_words(nc, w1_words, w1_sb, slice(2, 3))
         nc.sync.dma_start(out=b2_rows[0:bias_rows, :], in_=b2.rearrange("g (j m) -> (g j) m", m=P))
         load_scales(nc, w2_scales, w2_planes)
         load_words(nc, w2_words, w2_sb, slice(0, NETS))
@@ -183,11 +184,13 @@ def tile_lstmcellunknowndata_pa_e_kernel(
         quantise_hx(1)
         first_layer_tanh(0, 0, PAIR)
         first_layer_tanh(0, PAIR, PAIR)
+        first_layer_tanh(1, 0, HALF)
         quantise_hx(2)
         quantise_hx(3)
         b2_cols = bias_columns(b2_rows, "b2_cols")
         quantise_a(0, 0)
-        for h, g in ((0, 1), (0, 2), (1, 0), (1, 1), (1, 2)):
+        quantise_a(0, 1)
+        for h, g in ((0, 2), (1, 0), (1, 1), (1, 2)):
             first_layer_tanh(g, h * HALF, HALF)
             quantise_a(h, g)
 

from contextlib import ExitStack

import concourse.mybir as mybir
from concourse.masks import make_identity

F32 = mybir.dt.float32
BF16 = mybir.dt.bfloat16
I32 = mybir.dt.int32
U32 = mybir.dt.uint32
U8 = mybir.dt.uint8
FP8X4 = mybir.dt.float8_e4m3fn_x4
FUNC = mybir.ActivationFunctionType
ALU = mybir.AluOpType

P = 128
PACK = 4
BATCH = 1024
WIDTH = 512
NETS = 3
TILES = BATCH // P
HALVES = 2
HALF = BATCH // HALVES
TILES_PER_HALF = TILES // HALVES
PAIR = 2 * P
SLICES = WIDTH // P
QUADRANTS = 4
CHUNKS = HALVES * SLICES

FLOPS = 2 * 2 * NETS * BATCH * WIDTH * WIDTH


def load_scales(nc, scales_dram, planes):
    for quadrant in range(QUADRANTS):
        rows = slice(PACK * quadrant, PACK * quadrant + PACK)
        nc.sync.dma_start(
            out=planes[32 * quadrant : 32 * quadrant + PACK, :, :].bitcast(I32),
            in_=scales_dram[:, rows, :].rearrange("g r n -> r g n").bitcast(I32),
        )


def load_words(nc, words_dram, words, nets):
    nc.sync.dma_start(
        out=words[:, nets, :].bitcast(I32),
        in_=words_dram[nets].rearrange("g p n t -> p g (n t)").bitcast(I32),
    )


def tile_lstmcellunknowndata_pa_e_kernel(
    tc, hx, cx2, w1_words, w1_scales, b1, w2_words, w2_scales, b2, out
):
    nc = tc.nc
    with ExitStack() as stack:
        keep = stack.enter_context(tc.tile_pool(name="keep", bufs=1))
        stage = stack.enter_context(tc.tile_pool(name="stage", bufs=2))
        rows_pool = stack.enter_context(tc.tile_pool(name="rows", bufs=12))
        planes_pool = stack.enter_context(tc.tile_pool(name="planes", bufs=4))
        work = stack.enter_context(tc.tile_pool(name="work", bufs=4))
        psum_sums = stack.enter_context(tc.psum_pool(name="psum_sums", bufs=4))
        psum_turn = stack.enter_context(tc.psum_pool(name="psum_turn", bufs=4))
        stack.enter_context(tc.manual_schedule())

        w1_sb = keep.tile([P, NETS, WIDTH], U32, align_bytes=64)
        w1_planes = keep.tile([P, NETS, WIDTH], U8, align_bytes=64)
        w2_sb = keep.tile([P, NETS, WIDTH], U32, align_bytes=64)
        w2_planes = keep.tile([P, NETS, WIDTH], U8, align_bytes=64)
        b1_rows = keep.tile([P, P], BF16)
        b2_rows = keep.tile([P, P], BF16)
        warm = keep.tile([P, 1], F32)
        nc.vector.memset(w1_planes[:].rearrange("p g n -> p (g n)").bitcast(I32), 0)
        nc.vector.memset(b1_rows[:], 0.0)
        nc.vector.memset(warm[:], 0.0)
        nc.vector.memset(b2_rows[:], 0.0)
        nc.vector.memset(w2_planes[:].rearrange("p g n -> p (g n)").bitcast(I32), 0)

        ident_f32 = keep.tile([P, P], F32)
        make_identity(nc, ident_f32[:])
        ident_bf16 = keep.tile([P, P], BF16)
        make_identity(nc, ident_bf16[:])

        hx_view = hx.rearrange("(p i) k -> p i k", i=TILES)
        cx_view = cx2.rearrange("(p i) k -> p i k", i=TILES)
        out_view = out.rearrange("(p i) k -> p i k", i=TILES)
        x_sb = keep.tile([P, TILES, WIDTH], BF16)
        cx_sb = keep.tile([P, TILES, WIDTH], BF16)
        bias_rows = NETS * SLICES

        nc.scalar.dma_start(out=x_sb[:, 0:2, :], in_=hx_view[:, 0:2, :])
        nc.scalar.dma_start(out=x_sb[:, 2:4, :], in_=hx_view[:, 2:4, :])
        load_scales(nc, w1_scales, w1_planes)
        load_words(nc, w1_words, w1_sb, slice(0, 1))
        nc.scalar.dma_start(out=b1_rows[0:bias_rows, :], in_=b1.rearrange("g (j m) -> (g j) m", m=P))
        load_words(nc, w1_words, w1_sb, slice(1, 2))
        nc.sync.dma_start(out=x_sb[:, 4:8, :], in_=hx_view[:, 4:8, :])
        load_words(nc, w1_words, w1_sb, slice(2, 3))
        nc.sync.dma_start(out=b2_rows[0:bias_rows, :], in_=b2.rearrange("g (j m) -> (g j) m", m=P))
        load_scales(nc, w2_scales, w2_planes)
        load_words(nc, w2_words, w2_sb, slice(0, NETS))
        nc.gpsimd.dma_start(out=cx_sb[:], in_=cx_view)

        nc.scalar.activation(out=warm[:], in_=warm[:], func=FUNC.Sigmoid)

        hx_codes = keep.tile([P, BATCH], U32, align_bytes=64)
        hx_scales = keep.tile([P, BATCH], U8, align_bytes=64)

        def quantise_hx(pair):
            xt = psum_turn.tile([P, 2, 2, P], F32, tag="turn")
            for il in range(2):
                x_words = x_sb[:, 2 * pair + il, :].bitcast(F32)
                for u in range(2):
                    nc.tensor.transpose(
                        out=xt[:, il, u, :],
                        in_=x_words[:, u : WIDTH // 2 : 2],
                        identity=ident_f32[:],
                    )
            x_grouped = stage.tile([P, PAIR, PACK], BF16, align_bytes=64)
            nc.vector.tensor_copy(
                out=x_grouped[:]
                .rearrange("p c t -> p (c t)")
                .bitcast(F32)
                .rearrange("p (i c u) -> p i c u", i=2, u=2),
                in_=xt[:].rearrange("p i u c -> p i c u"),
            )
            cols = slice(pair * PAIR, (pair + 1) * PAIR)
            nc.vector.quantize_mx(
                out=hx_codes[:, cols].bitcast(FP8X4),
                scales=hx_scales[:, cols],
                in_=x_grouped[:].rearrange("p c t -> p (c t)"),
            )

        def bias_columns(rows, name):
            turned = psum_turn.tile([P, P], BF16, tag="turn")
            nc.tensor.transpose(out=turned[:], in_=rows[:], identity=ident_bf16[:])
            columns = keep.tile([P, bias_rows], F32, name=name)
            nc.vector.tensor_copy(out=columns[:], in_=turned[:, 0:bias_rows])
            return columns

        a_codes = keep.tile([P, NETS, BATCH], U32, align_bytes=64)
        a_scales = keep.tile([P, NETS, BATCH], U8, align_bytes=64)
        a_planes_of = {}

        def first_layer_tanh(g, first_col, n_cols):
            h = first_col // HALF
            if (h, g) not in a_planes_of:
                a_planes_of[(h, g)] = planes_pool.tile([P, PACK, HALF], BF16, name="a_planes")
            a_planes = a_planes_of[(h, g)]
            cols = slice(first_col, first_col + n_cols)
            cols_in_half = slice(first_col - h * HALF, first_col - h * HALF + n_cols)
            for j in range(SLICES):
                units = slice(j * P, (j + 1) * P)
                h1 = psum_sums.tile([P, n_cols], F32, tag="sums")
                nc.tensor.matmul_mx(
                    out=h1[:],
                    lhsT=w1_sb[:, g, units].bitcast(FP8X4),
                    lhsT_scale=w1_planes[:, g, units],
                    rhs=hx_codes[:, cols].bitcast(FP8X4),
                    rhs_scale=hx_scales[:, cols],
                    start=True,
                    stop=True,
                )
                a_rows = rows_pool.tile([P, n_cols], BF16, tag="a_rows")
                column = g * SLICES + j
                nc.scalar.activation(
                    out=a_rows[:], in_=h1[:], func=FUNC.Tanh, bias=b1_cols[:, column : column + 1]
                )
                nc.sync.dma_start(
                    out=a_planes[32 * j : 32 * j + 32, :, cols_in_half], in_=a_rows[:]
                )

        def quantise_a(h, g):
            cols = slice(h * HALF, (h + 1) * HALF)
            a_grouped = stage.tile([P, HALF, PACK], BF16, align_bytes=64)
            nc.vector.tensor_copy(
                out=a_grouped[:].rearrange("p (c i) t -> p c t i", i=4),
                in_=a_planes_of[(h, g)][:].rearrange("p t (c i) -> p c t i", i=4),
            )
            nc.vector.quantize_mx(
                out=a_codes[:, g, cols].bitcast(FP8X4),
                scales=a_scales[:, g, cols],
                in_=a_grouped[:].rearrange("p c t -> p (c t)"),
            )

        quantise_hx(0)
        b1_cols = bias_columns(b1_rows, "b1_cols")
        quantise_hx(1)
        first_layer_tanh(0, 0, PAIR)
        first_layer_tanh(0, PAIR, PAIR)
        first_layer_tanh(1, 0, HALF)
        quantise_hx(2)
        quantise_hx(3)
        b2_cols = bias_columns(b2_rows, "b2_cols")
        quantise_a(0, 0)
        quantise_a(0, 1)
        for h, g in ((0, 2), (1, 0), (1, 1), (1, 2)):
            first_layer_tanh(g, h * HALF, HALF)
            quantise_a(h, g)

        turned_tanh_of = {}
        gates_of = {}
        cell_of = {}

        def second_layer_tanh(chunk):
            h, j = divmod(chunk, SLICES)
            cols = slice(h * HALF, (h + 1) * HALF)
            units = slice(j * P, (j + 1) * P)
            turned_tanh = work.tile([P, NETS, HALF], F32, name="turned_tanh")
            turned_tanh_of[chunk] = turned_tanh
            for g in range(NETS):
                h2 = psum_sums.tile([P, HALF], F32, tag="sums")
                nc.tensor.matmul_mx(
                    out=h2[:],
                    lhsT=w2_sb[:, g, units].bitcast(FP8X4),
                    lhsT_scale=w2_planes[:, g, units],
                    rhs=a_codes[:, g, cols].bitcast(FP8X4),
                    rhs_scale=a_scales[:, g, cols],
                    start=True,
                    stop=True,
                )
                column = g * SLICES + j
                nc.scalar.activation(
                    out=turned_tanh[:, g, :],
                    in_=h2[:],
                    func=FUNC.Tanh,
                    bias=b2_cols[:, column : column + 1],
                )

        def turn_back_and_sigmoid(chunk):
            h, j = divmod(chunk, SLICES)
            turned_tanh = turned_tanh_of[chunk]
            gates = work.tile([P, NETS, TILES_PER_HALF, P], F32, name="gates")
            gates_of[chunk] = gates
            for g in reversed(range(NETS)):
                back = psum_turn.tile([P, TILES_PER_HALF, P], F32, tag="turn")
                for il in range(TILES_PER_HALF):
                    nc.tensor.transpose(
                        out=back[:, il, :],
                        in_=turned_tanh[:, g, il * P : (il + 1) * P],
                        identity=ident_f32[:],
                    )
                nc.scalar.activation(out=gates[:, g, :, :], in_=back[:], func=FUNC.Sigmoid)
            cell = work.tile([P, TILES_PER_HALF, P], F32, name="cell")
            cell_of[chunk] = cell
            tiles = slice(h * TILES_PER_HALF, (h + 1) * TILES_PER_HALF)
            nc.vector.tensor_tensor(
                out=cell[:],
                in0=gates[:, 1, :, :],
                in1=cx_sb[:, tiles, j * P : (j + 1) * P],
                op=ALU.mult,
            )

        def finish(chunk):
            h, j = divmod(chunk, SLICES)
            gates = gates_of[chunk]
            cell = cell_of[chunk]
            candidate = work.tile([P, TILES_PER_HALF, P], F32)
            nc.scalar.activation(out=candidate[:], in_=gates[:, 2, :, :], func=FUNC.Tanh)
            nc.vector.tensor_tensor(
                out=candidate[:], in0=gates[:, 0, :, :], in1=candidate[:], op=ALU.mult
            )
            nc.vector.tensor_tensor(out=cell[:], in0=cell[:], in1=candidate[:], op=ALU.add)
            tiles = slice(h * TILES_PER_HALF, (h + 1) * TILES_PER_HALF)
            nc.sync.dma_start(out=out_view[:, tiles, j * P : (j + 1) * P], in_=cell[:])

        for step in range(CHUNKS + 2):
            if step >= 2:
                finish(step - 2)
            if step < CHUNKS:
                second_layer_tanh(step)
            if 1 <= step <= CHUNKS:
                turn_back_and_sigmoid(step - 1)
